import numpy as np
import ml_dtypes


def mxq(x, axis, fmt="e4m3"):
    dtype, down = {"e4m3": (ml_dtypes.float8_e4m3fn, 7), "e5m2": (ml_dtypes.float8_e5m2, 14)}[fmt]
    v = np.moveaxis(np.asarray(x, np.float32).astype(ml_dtypes.bfloat16).astype(np.float64), axis, -1)
    blocks = v.reshape(v.shape[:-1] + (-1, 32))
    amax = np.abs(blocks).max(-1, keepdims=True)
    byte = np.maximum(np.where(amax > 0, np.frexp(amax)[1] - 1 + 127, 0) - down, 1)
    scale = np.exp2(byte - 127.0)
    codes = (blocks / scale).astype(np.float32).astype(dtype).astype(np.float64)
    return np.moveaxis((codes * scale).reshape(v.shape), -1, axis)


WIDE = False


def mx_kscale(k):
    if not WIDE:
        return np.ones(k)
    levels = np.array([10, -10, 5, -5, 0])
    a = np.random.permutation(np.resize(levels, k // 512 * 4)).reshape(k // 512, 4)
    idx = np.arange(k)
    return np.exp2(a[idx // 512, idx % 128 // 32])


BF16 = ml_dtypes.bfloat16


def bf(x):
    return np.asarray(x, np.float32).astype(BF16)


def f64(x):
    return np.asarray(x).astype(np.float64)


M, K, N = 8192, 1024, 512


def binarize(v):
    clipped = np.clip(v, -1.0, 1.0)
    rounded = np.sign(clipped)
    return clipped + (rounded - clipped)


def setup_inputs():
    s = mx_kscale(K)
    keep = (s <= s.min() * 4.0).astype(np.float64)
    return {"x": bf(np.random.standard_normal((M, K)) * (s / s.min())[None, :]),
            "w": bf(np.random.standard_normal((K, N)) / np.sqrt(K) * keep[:, None]),
            "gamma": bf(-(1.0 + 0.1 * np.random.standard_normal(1)) / np.sqrt(keep.sum()))}


def reference(x, w, gamma):
    clamped_w = np.abs(f64(gamma)) * binarize(f64(w))
    return mxq(f64(x), 1, "e4m3") @ mxq(clamped_w, 0, "e4m3")

@@ -1,0 +1,212 @@
+from contextlib import ExitStack
+
+import concourse.mybir as mybir
+from concourse.masks import make_identity
+
+F32 = mybir.dt.float32
+BF16 = mybir.dt.bfloat16
+U32 = mybir.dt.uint32
+U8 = mybir.dt.uint8
+FP8X4 = mybir.dt.float8_e4m3fn_x4
+ACT = mybir.ActivationFunctionType
+ALU = mybir.AluOpType
+
+M, K, N = 8192, 1024, 512
+FLOPS = 2 * M * K * N
+
+P = 128
+TILES = M // P
+R = 4
+ROUNDS = TILES // R
+WORDS = K // 2
+CHUNKS = (2, 2, 4, 8, 8, 8, 8, 8, 8, 8)
+HALF = 256
+
+
+def tile_binary_dense_t_kernel(tc, x, w, gamma, out):
+    nc = tc.nc
+    xv = x.rearrange("(p t) k -> p (t k)", t=TILES)
+    ov = out.rearrange("(p t) n -> p (t n)", t=TILES)
+    wv = w.rearrange("(g u p e) n -> p g u e n", g=2, u=2, p=P, e=2)
+
+    with ExitStack() as ctx:
+        const = ctx.enter_context(tc.tile_pool(name="const", bufs=1))
+        xpool = ctx.enter_context(tc.tile_pool(name="xpool", bufs=1))
+        stage = ctx.enter_context(tc.tile_pool(name="stage", bufs=7))
+        gpool = ctx.enter_context(tc.tile_pool(name="gpool", bufs=2))
+        qpool = ctx.enter_context(tc.tile_pool(name="qpool", bufs=3))
+        psum_t = ctx.enter_context(tc.psum_pool(name="psum_t", bufs=4))
+        psum_o = ctx.enter_context(tc.psum_pool(name="psum_o", bufs=4))
+        ctx.enter_context(tc.manual_schedule())
+
+        ident = const.tile([P, P], F32, name="ident")
+        make_identity(nc, ident[:])
+
+        g_bf = const.tile([P, 1], BF16, name="g_bf")
+        nc.scalar.dma_start(out=g_bf[:], in_=gamma.partition_broadcast(P))
+
+        w_raw = stage.tile([P, 2, 4, N], BF16, name="w_raw", tag="stage", align_bytes=64)
+        x_words = []
+
+        def load_w(g):
+            nc.sync.dma_start(
+                out=w_raw[:, g].rearrange("p (u e) n -> p u e n", e=2), in_=wv[:, g]
+            )
+
+        def load_x(c):
+            first = sum(CHUNKS[:c])
+            x_sb = xpool.tile([P, CHUNKS[c] * K], BF16, name="x%d" % c)
+            nc.sync.dma_start(out=x_sb[:], in_=xv[:, first * K : (first + CHUNKS[c]) * K])
+            for i in range(CHUNKS[c]):
+                x_words.append((x_sb[:].bitcast(F32), i * WORDS))
+
+        load_w(0)
+        load_x(0)
+        load_w(1)
+        for c in range(1, len(CHUNKS)):
+            load_x(c)
+
+        absg = const.tile([P, 1], F32, name="absg")
+        nc.scalar.activation(out=absg[:], in_=g_bf[:], func=ACT.Abs)
+
+        sg = stage.tile([P, 2, 4, N], BF16, name="sg", tag="stage", align_bytes=64)
+        wg = stage.tile([P, 2, N, 4], BF16, name="wg", tag="stage", align_bytes=64)
+        w_codes = const.tile([P, 2 * N], U32, name="w_codes", align_bytes=64)
+        w_scales = const.tile([P, 2 * N], U8, name="w_scales", align_bytes=64)
+
+        def w_sign(g, h):
+            cols = slice(h * HALF, (h + 1) * HALF)
+            nc.scalar.activation(out=sg[:, g, :, cols], in_=w_raw[:, g, :, cols], func=ACT.Sign)
+
+        def w_group(g, h):
+            cols = slice(h * HALF, (h + 1) * HALF)
+            nc.vector.tensor_scalar(
+                out=wg[:, g, cols, :].rearrange("p (c i) t -> p c t i", i=4),
+                in0=sg[:, g, :, cols].rearrange("p t (c i) -> p c t i", i=4),
+                scalar1=absg[:, 0:1],
+                scalar2=None,
+                op0=ALU.mult,
+            )
+
+        def w_quant(g):
+            nc.vector.quantize_mx(
+                out=w_codes[:, g * N : (g + 1) * N].bitcast(FP8X4),
+                scales=w_scales[:, g * N : (g + 1) * N],
+                in_=wg[:, g].rearrange("p n t -> p (n t)"),
+            )
+
+        banks = {}
+        grouped = {}
+        codes = {}
+        scales = {}
+
+        def transposes(r, pool, tag):
+            for i in range(R):
+                xt = pool.tile([P, 2, 2, P], F32, name="xt_%d_%d" % (r, i), tag=tag)
+                words, first = x_words[r * R + i]
+                for j in range(4):
+                    nc.tensor.transpose(
+                        xt[:, j // 2, j % 2, :],
+                        words[:, first + j * P : first + (j + 1) * P],
+                        ident[:],
+                    )
+                banks[(r, i)] = xt
+
+        def copy_t(r, i, engine_copy):
+            if r not in grouped:
+                grouped[r] = gpool.tile(
+                    [P, R * K], BF16, name="grouped_%d" % r, tag="grouped", align_bytes=64
+                )
+            dst = grouped[r][:].bitcast(F32)[:, i * WORDS : (i + 1) * WORDS]
+            engine_copy(
+                out=dst.rearrange("p (g m u) -> p g m u", g=2, m=P, u=2),
+                in_=banks[(r, i)][:].rearrange("p g u m -> p g m u"),
+            )
+
+        def quant(r, first, count):
+            if r not in codes:
+                codes[r] = qpool.tile([P, R * 2 * P], U32, name="codes_%d" % r, tag="codes", align_bytes=64)
+                scales[r] = qpool.tile([P, R * 2 * P], U8, name="scales_%d" % r, tag="scales", align_bytes=64)
+            cols = slice(first * 2 * P, (first + count) * 2 * P)
+            nc.vector.quantize_mx(
+                out=codes[r][:, cols].bitcast(FP8X4),
+                scales=scales[r][:, cols],
+                in_=grouped[r][:, first * K : (first + count) * K],
+            )
+
+        accs = {}
+
+        def passes(r):
+            for i in range(R):
+                acc = psum_o.tile([P, N], F32, name="acc_%d_%d" % (r, i), tag="acc")
+                for g in range(2):
+                    cols = slice((i * 2 + g) * P, (i * 2 + g + 1) * P)
+                    nc.tensor.matmul_mx(
+                        out=acc[:],
+                        lhsT=codes[r][:, cols].bitcast(FP8X4),
+                        lhsT_scale=scales[r][:, cols],
+                        rhs=w_codes[:, g * N : (g + 1) * N].bitcast(FP8X4),
+                        rhs_scale=w_scales[:, g * N : (g + 1) * N],
+                        start=(g == 0),
+                        stop=(g == 1),
+                    )
+                accs[(r, i)] = acc
+
+        outs = {}
+
+        def copy_o(r, i, engine_copy):
+            if r not in outs:
+                outs[r] = stage.tile([P, R * N], F32, name="o_%d" % r, tag="stage", align_bytes=64)
+            engine_copy(out=outs[r][:, i * N : (i + 1) * N], in_=accs[(r, i)][:])
+
+        def store(r, first, count, queue):
+            t0 = r * R + first
+            queue.dma_start(
+                out=ov[:, t0 * N : (t0 + count) * N],
+                in_=outs[r][:, first * N : (first + count) * N],
+            )
+
+        vcopy = nc.vector.tensor_copy
+        scopy = nc.scalar.copy
+
+        transposes(0, psum_o, "acc")
+        w_sign(0, 0)
+        w_sign(0, 1)
+        w_sign(1, 0)
+        w_sign(1, 1)
+        w_group(0, 0)
+        w_group(0, 1)
+        copy_t(0, 0, vcopy)
+        w_quant(0)
+        w_group(1, 0)
+        copy_t(0, 1, vcopy)
+        w_group(1, 1)
+        quant(0, 0, 2)
+        w_quant(1)
+        copy_t(0, 2, scopy)
+        copy_t(0, 3, scopy)
+        quant(0, 2, 2)
+
+        for r in range(ROUNDS):
+            last = r == ROUNDS - 1
+            if not last:
+                transposes(r + 1, psum_t, "xt")
+                copy_t(r + 1, 0, scopy)
+                copy_t(r + 1, 1, vcopy)
+                copy_t(r + 1, 2, scopy)
+                copy_t(r + 1, 3, vcopy)
+            passes(r)
+            if not last:
+                copy_o(r, 0, vcopy)
+                copy_o(r, 1, scopy)
+                copy_o(r, 2, scopy)
+                copy_o(r, 3, scopy)
+                store(r, 0, R, nc.gpsimd)
+                quant(r + 1, 0, R)
+            else:
+                copy_o(r, 0, vcopy)
+                copy_o(r, 1, scopy)
+                store(r, 0, 2, nc.sync)
+                copy_o(r, 2, vcopy)
+                copy_o(r, 3, scopy)
+                store(r, 2, 2, nc.sync)

@@ -20,6 +20,8 @@ R = 4
 ROUNDS = TILES // R
 WORDS = K // 2
 CHUNKS = (2, 2, 4, 8, 8, 8, 8, 8, 8, 8)
+SMALL = 3
+BIG = 8
 HALF = 256
 
 
@@ -32,8 +34,8 @@ def tile_binary_dense_t_kernel(tc, x, w, gamma, out):
     with ExitStack() as ctx:
         const = ctx.enter_context(tc.tile_pool(name="const", bufs=1))
         xpool = ctx.enter_context(tc.tile_pool(name="xpool", bufs=1))
-        stage = ctx.enter_context(tc.tile_pool(name="stage", bufs=7))
-        gpool = ctx.enter_context(tc.tile_pool(name="gpool", bufs=2))
+        big = ctx.enter_context(tc.tile_pool(name="big", bufs=10))
+        gpool = ctx.enter_context(tc.tile_pool(name="gpool", bufs=3))
         qpool = ctx.enter_context(tc.tile_pool(name="qpool", bufs=3))
         psum_t = ctx.enter_context(tc.psum_pool(name="psum_t", bufs=4))
         psum_o = ctx.enter_context(tc.psum_pool(name="psum_o", bufs=4))
@@ -45,7 +47,9 @@ def tile_binary_dense_t_kernel(tc, x, w, gamma, out):
         g_bf = const.tile([P, 1], BF16, name="g_bf")
         nc.scalar.dma_start(out=g_bf[:], in_=gamma.partition_broadcast(P))
 
-        w_raw = stage.tile([P, 2, 4, N], BF16, name="w_raw", tag="stage", align_bytes=64)
+        w_tmp = big.tile([P, 2, 2, 4, N], BF16, name="w_tmp", tag="big", align_bytes=64)
+        w_raw = w_tmp[:, 0]
+        sg = w_tmp[:, 1]
         x_words = []
 
         def load_w(g):
@@ -55,7 +59,10 @@ def tile_binary_dense_t_kernel(tc, x, w, gamma, out):
 
         def load_x(c):
             first = sum(CHUNKS[:c])
-            x_sb = xpool.tile([P, CHUNKS[c] * K], BF16, name="x%d" % c)
+            if c < SMALL:
+                x_sb = xpool.tile([P, CHUNKS[c] * K], BF16, name="x%d" % c)
+            else:
+                x_sb = big.tile([P, BIG * K], BF16, name="x%d" % c, tag="big", align_bytes=64)
             nc.sync.dma_start(out=x_sb[:], in_=xv[:, first * K : (first + CHUNKS[c]) * K])
             for i in range(CHUNKS[c]):
                 x_words.append((x_sb[:].bitcast(F32), i * WORDS))
@@ -69,8 +76,7 @@ def tile_binary_dense_t_kernel(tc, x, w, gamma, out):
         absg = const.tile([P, 1], F32, name="absg")
         nc.scalar.activation(out=absg[:], in_=g_bf[:], func=ACT.Abs)
 
-        sg = stage.tile([P, 2, 4, N], BF16, name="sg", tag="stage", align_bytes=64)
-        wg = stage.tile([P, 2, N, 4], BF16, name="wg", tag="stage", align_bytes=64)
+        wg = gpool.tile([P, 2, N, 4], BF16, name="wg", tag="grouped", align_bytes=64)
         w_codes = const.tile([P, 2 * N], U32, name="w_codes", align_bytes=64)
         w_scales = const.tile([P, 2 * N], U8, name="w_scales", align_bytes=64)
 
@@ -155,15 +161,17 @@ def tile_binary_dense_t_kernel(tc, x, w, gamma, out):
         outs = {}
 
         def copy_o(r, i, engine_copy):
-            if r not in outs:
-                outs[r] = stage.tile([P, R * N], F32, name="o_%d" % r, tag="stage", align_bytes=64)
-            engine_copy(out=outs[r][:, i * N : (i + 1) * N], in_=accs[(r, i)][:])
+            t = r * R + i
+            if t // BIG not in outs:
+                outs[t // BIG] = big.tile(
+                    [P, BIG * N], F32, name="o_%d" % (t // BIG), tag="big", align_bytes=64
+                )
+            engine_copy(out=outs[t // BIG][:, (t % BIG) * N : (t % BIG + 1) * N], in_=accs[(r, i)][:])
 
-        def store(r, first, count, queue):
-            t0 = r * R + first
-            queue.dma_start(
+        def store(t0, count):
+            nc.sync.dma_start(
                 out=ov[:, t0 * N : (t0 + count) * N],
-                in_=outs[r][:, first * N : (first + count) * N],
+                in_=outs[t0 // BIG][:, (t0 % BIG) * N : (t0 % BIG + count) * N],
             )
 
         vcopy = nc.vector.tensor_copy
@@ -201,12 +209,15 @@ def tile_binary_dense_t_kernel(tc, x, w, gamma, out):
                 copy_o(r, 1, scopy)
                 copy_o(r, 2, scopy)
                 copy_o(r, 3, scopy)
-                store(r, 0, R, nc.gpsimd)
+                if r == ROUNDS - 2:
+                    store(r * R, R)
+                elif r % 2 == 1:
+                    store((r - 1) * R, BIG)
                 quant(r + 1, 0, R)
             else:
                 copy_o(r, 0, vcopy)
                 copy_o(r, 1, scopy)
-                store(r, 0, 2, nc.sync)
+                store(r * R, 2)
                 copy_o(r, 2, vcopy)
                 copy_o(r, 3, scopy)
-                store(r, 2, 2, nc.sync)
+                store(r * R + 2, 2)

@@ -44,8 +44,11 @@ def tile_binary_dense_t_kernel(tc, x, w, gamma, out):
         ident = const.tile([P, P], F32, name="ident")
         make_identity(nc, ident[:])
 
-        g_bf = const.tile([P, 1], BF16, name="g_bf")
-        nc.scalar.dma_start(out=g_bf[:], in_=gamma.partition_broadcast(P))
+        g_row = const.tile([P, 2], BF16, name="g_row")
+        nc.vector.memset(g_row[:], 0.0)
+        nc.scalar.dma_start(out=g_row[0:1, 0:1], in_=gamma.partition_broadcast(1))
+        ones = const.tile([P, P], BF16, name="ones")
+        nc.vector.memset(ones[:], 1.0)
 
         w_tmp = big.tile([P, 2, 2, 4, N], BF16, name="w_tmp", tag="big", align_bytes=64)
         w_raw = w_tmp[:, 0]
@@ -73,8 +76,9 @@ def tile_binary_dense_t_kernel(tc, x, w, gamma, out):
         for c in range(1, len(CHUNKS)):
             load_x(c)
 
+        g_ps = psum_t.tile([P, N], F32, name="g_ps", tag="xt")
+        nc.tensor.matmul(g_ps[:, 0:2], lhsT=ones[:], rhs=g_row[:], start=True, stop=True)
         absg = const.tile([P, 1], F32, name="absg")
-        nc.scalar.activation(out=absg[:], in_=g_bf[:], func=ACT.Abs)
 
         wg = gpool.tile([P, 2, N, 4], BF16, name="wg", tag="grouped", align_bytes=64)
         w_codes = const.tile([P, 2 * N], U32, name="w_codes", align_bytes=64)
@@ -179,6 +183,7 @@ def tile_binary_dense_t_kernel(tc, x, w, gamma, out):
 
         transposes(0, psum_o, "acc")
         w_sign(0, 0)
+        nc.scalar.activation(out=absg[:], in_=g_ps[:, 0:1], func=ACT.Abs)
         w_sign(0, 1)
         w_sign(1, 0)
         w_sign(1, 1)

@@ -212,17 +212,18 @@ def tile_binary_dense_t_kernel(tc, x, w, gamma, out):
             if not last:
                 copy_o(r, 0, vcopy)
                 copy_o(r, 1, scopy)
+                if r == ROUNDS - 2:
+                    store(r * R, 2)
                 copy_o(r, 2, scopy)
                 copy_o(r, 3, scopy)
                 if r == ROUNDS - 2:
+                    store(r * R + 2, 2)
+                elif r >= ROUNDS // 2:
                     store(r * R, R)
                 elif r % 2 == 1:
                     store((r - 1) * R, BIG)
                 quant(r + 1, 0, R)
             else:
-                copy_o(r, 0, vcopy)
-                copy_o(r, 1, scopy)
-                store(r * R, 2)
-                copy_o(r, 2, vcopy)
-                copy_o(r, 3, scopy)
-                store(r * R + 2, 2)
+                for i in range(R):
+                    copy_o(r, i, scopy if i % 2 else vcopy)
+                    store(r * R + i, 1)

@@ -27,8 +27,8 @@ HALF = 256
 
 def tile_binary_dense_t_kernel(tc, x, w, gamma, out):
     nc = tc.nc
-    xv = x.rearrange("(p t) k -> p (t k)", t=TILES)
-    ov = out.rearrange("(p t) n -> p (t n)", t=TILES)
+    xv = x.rearrange("(b p t) k -> b p (t k)", p=P, t=BIG)
+    ov = out.rearrange("(b p t) n -> b p (t n)", p=P, t=BIG)
     wv = w.rearrange("(g u p e) n -> p g u e n", g=2, u=2, p=P, e=2)
 
     with ExitStack() as ctx:
@@ -66,7 +66,10 @@ def tile_binary_dense_t_kernel(tc, x, w, gamma, out):
                 x_sb = xpool.tile([P, CHUNKS[c] * K], BF16, name="x%d" % c)
             else:
                 x_sb = big.tile([P, BIG * K], BF16, name="x%d" % c, tag="big", align_bytes=64)
-            nc.sync.dma_start(out=x_sb[:], in_=xv[:, first * K : (first + CHUNKS[c]) * K])
+            t = first % BIG
+            nc.sync.dma_start(
+                out=x_sb[:], in_=xv[first // BIG][:, t * K : (t + CHUNKS[c]) * K]
+            )
             for i in range(CHUNKS[c]):
                 x_words.append((x_sb[:].bitcast(F32), i * WORDS))
 
@@ -174,7 +177,7 @@ def tile_binary_dense_t_kernel(tc, x, w, gamma, out):
 
         def store(t0, count):
             nc.sync.dma_start(
-                out=ov[:, t0 * N : (t0 + count) * N],
+                out=ov[t0 // BIG][:, (t0 % BIG) * N : (t0 % BIG + count) * N],
                 in_=outs[t0 // BIG][:, (t0 % BIG) * N : (t0 % BIG + count) * N],
             )
 

@@ -46,7 +46,6 @@ def tile_binary_dense_t_kernel(tc, x, w, gamma, out):
 
         g_row = const.tile([P, 2], BF16, name="g_row")
         nc.vector.memset(g_row[:], 0.0)
-        nc.scalar.dma_start(out=g_row[0:1, 0:1], in_=gamma.partition_broadcast(1))
         ones = const.tile([P, P], BF16, name="ones")
         nc.vector.memset(ones[:], 1.0)
 
@@ -75,6 +74,7 @@ def tile_binary_dense_t_kernel(tc, x, w, gamma, out):
 
         load_w(0)
         load_x(0)
+        nc.sync.dma_start(out=g_row[0:1, 0:1], in_=gamma.partition_broadcast(1))
         load_w(1)
         for c in range(1, len(CHUNKS)):
             load_x(c)

from contextlib import ExitStack

import concourse.mybir as mybir
from concourse.masks import make_identity

F32 = mybir.dt.float32
BF16 = mybir.dt.bfloat16
U32 = mybir.dt.uint32
U8 = mybir.dt.uint8
FP8X4 = mybir.dt.float8_e4m3fn_x4
ACT = mybir.ActivationFunctionType
ALU = mybir.AluOpType

M, K, N = 8192, 1024, 512
FLOPS = 2 * M * K * N

P = 128
TILES = M // P
R = 4
ROUNDS = TILES // R
WORDS = K // 2
CHUNKS = (2, 2, 4, 8, 8, 8, 8, 8, 8, 8)
SMALL = 3
BIG = 8
HALF = 256


def tile_binary_dense_t_kernel(tc, x, w, gamma, out):
    nc = tc.nc
    xv = x.rearrange("(b p t) k -> b p (t k)", p=P, t=BIG)
    ov = out.rearrange("(b p t) n -> b p (t n)", p=P, t=BIG)
    wv = w.rearrange("(g u p e) n -> p g u e n", g=2, u=2, p=P, e=2)

    with ExitStack() as ctx:
        const = ctx.enter_context(tc.tile_pool(name="const", bufs=1))
        xpool = ctx.enter_context(tc.tile_pool(name="xpool", bufs=1))
        big = ctx.enter_context(tc.tile_pool(name="big", bufs=10))
        gpool = ctx.enter_context(tc.tile_pool(name="gpool", bufs=3))
        qpool = ctx.enter_context(tc.tile_pool(name="qpool", bufs=3))
        psum_t = ctx.enter_context(tc.psum_pool(name="psum_t", bufs=4))
        psum_o = ctx.enter_context(tc.psum_pool(name="psum_o", bufs=4))
        ctx.enter_context(tc.manual_schedule())

        ident = const.tile([P, P], F32, name="ident")
        make_identity(nc, ident[:])

        g_row = const.tile([P, 2], BF16, name="g_row")
        nc.vector.memset(g_row[:], 0.0)
        ones = const.tile([P, P], BF16, name="ones")
        nc.vector.memset(ones[:], 1.0)

        w_tmp = big.tile([P, 2, 2, 4, N], BF16, name="w_tmp", tag="big", align_bytes=64)
        w_raw = w_tmp[:, 0]
        sg = w_tmp[:, 1]
        x_words = []

        def load_w(g):
            nc.sync.dma_start(
                out=w_raw[:, g].rearrange("p (u e) n -> p u e n", e=2), in_=wv[:, g]
            )

        def load_x(c):
            first = sum(CHUNKS[:c])
            if c < SMALL:
                x_sb = xpool.tile([P, CHUNKS[c] * K], BF16, name="x%d" % c)
            else:
                x_sb = big.tile([P, BIG * K], BF16, name="x%d" % c, tag="big", align_bytes=64)
            t = first % BIG
            nc.sync.dma_start(
                out=x_sb[:], in_=xv[first // BIG][:, t * K : (t + CHUNKS[c]) * K]
            )
            for i in range(CHUNKS[c]):
                x_words.append((x_sb[:].bitcast(F32), i * WORDS))

        load_w(0)
        load_x(0)
        nc.sync.dma_start(out=g_row[0:1, 0:1], in_=gamma.partition_broadcast(1))
        load_w(1)
        for c in range(1, len(CHUNKS)):
            load_x(c)

        g_ps = psum_t.tile([P, N], F32, name="g_ps", tag="xt")
        nc.tensor.matmul(g_ps[:, 0:2], lhsT=ones[:], rhs=g_row[:], start=True, stop=True)
        absg = const.tile([P, 1], F32, name="absg")

        wg = gpool.tile([P, 2, N, 4], BF16, name="wg", tag="grouped", align_bytes=64)
        w_codes = const.tile([P, 2 * N], U32, name="w_codes", align_bytes=64)
        w_scales = const.tile([P, 2 * N], U8, name="w_scales", align_bytes=64)

        def w_sign(g, h):
            cols = slice(h * HALF, (h + 1) * HALF)
            nc.scalar.activation(out=sg[:, g, :, cols], in_=w_raw[:, g, :, cols], func=ACT.Sign)

        def w_group(g, h):
            cols = slice(h * HALF, (h + 1) * HALF)
            nc.vector.tensor_scalar(
                out=wg[:, g, cols, :].rearrange("p (c i) t -> p c t i", i=4),
                in0=sg[:, g, :, cols].rearrange("p t (c i) -> p c t i", i=4),
                scalar1=absg[:, 0:1],
                scalar2=None,
                op0=ALU.mult,
            )

        def w_quant(g):
            nc.vector.quantize_mx(
                out=w_codes[:, g * N : (g + 1) * N].bitcast(FP8X4),
                scales=w_scales[:, g * N : (g + 1) * N],
                in_=wg[:, g].rearrange("p n t -> p (n t)"),
            )

        banks = {}
        grouped = {}
        codes = {}
        scales = {}

        def transposes(r, pool, tag):
            for i in range(R):
                xt = pool.tile([P, 2, 2, P], F32, name="xt_%d_%d" % (r, i), tag=tag)
                words, first = x_words[r * R + i]
                for j in range(4):
                    nc.tensor.transpose(
                        xt[:, j // 2, j % 2, :],
                        words[:, first + j * P : first + (j + 1) * P],
                        ident[:],
                    )
                banks[(r, i)] = xt

        def copy_t(r, i, engine_copy):
            if r not in grouped:
                grouped[r] = gpool.tile(
                    [P, R * K], BF16, name="grouped_%d" % r, tag="grouped", align_bytes=64
                )
            dst = grouped[r][:].bitcast(F32)[:, i * WORDS : (i + 1) * WORDS]
            engine_copy(
                out=dst.rearrange("p (g m u) -> p g m u", g=2, m=P, u=2),
                in_=banks[(r, i)][:].rearrange("p g u m -> p g m u"),
            )

        def quant(r, first, count):
            if r not in codes:
                codes[r] = qpool.tile([P, R * 2 * P], U32, name="codes_%d" % r, tag="codes", align_bytes=64)
                scales[r] = qpool.tile([P, R * 2 * P], U8, name="scales_%d" % r, tag="scales", align_bytes=64)
            cols = slice(first * 2 * P, (first + count) * 2 * P)
            nc.vector.quantize_mx(
                out=codes[r][:, cols].bitcast(FP8X4),
                scales=scales[r][:, cols],
                in_=grouped[r][:, first * K : (first + count) * K],
            )

        accs = {}

        def passes(r):
            for i in range(R):
                acc = psum_o.tile([P, N], F32, name="acc_%d_%d" % (r, i), tag="acc")
                for g in range(2):
                    cols = slice((i * 2 + g) * P, (i * 2 + g + 1) * P)
                    nc.tensor.matmul_mx(
                        out=acc[:],
                        lhsT=codes[r][:, cols].bitcast(FP8X4),
                        lhsT_scale=scales[r][:, cols],
                        rhs=w_codes[:, g * N : (g + 1) * N].bitcast(FP8X4),
                        rhs_scale=w_scales[:, g * N : (g + 1) * N],
                        start=(g == 0),
                        stop=(g == 1),
                    )
                accs[(r, i)] = acc

        outs = {}

        def copy_o(r, i, engine_copy):
            t = r * R + i
            if t // BIG not in outs:
                outs[t // BIG] = big.tile(
                    [P, BIG * N], F32, name="o_%d" % (t // BIG), tag="big", align_bytes=64
                )
            engine_copy(out=outs[t // BIG][:, (t % BIG) * N : (t % BIG + 1) * N], in_=accs[(r, i)][:])

        def store(t0, count):
            nc.sync.dma_start(
                out=ov[t0 // BIG][:, (t0 % BIG) * N : (t0 % BIG + count) * N],
                in_=outs[t0 // BIG][:, (t0 % BIG) * N : (t0 % BIG + count) * N],
            )

        vcopy = nc.vector.tensor_copy
        scopy = nc.scalar.copy

        transposes(0, psum_o, "acc")
        w_sign(0, 0)
        nc.scalar.activation(out=absg[:], in_=g_ps[:, 0:1], func=ACT.Abs)
        w_sign(0, 1)
        w_sign(1, 0)
        w_sign(1, 1)
        w_group(0, 0)
        w_group(0, 1)
        copy_t(0, 0, vcopy)
        w_quant(0)
        w_group(1, 0)
        copy_t(0, 1, vcopy)
        w_group(1, 1)
        quant(0, 0, 2)
        w_quant(1)
        copy_t(0, 2, scopy)
        copy_t(0, 3, scopy)
        quant(0, 2, 2)

        for r in range(ROUNDS):
            last = r == ROUNDS - 1
            if not last:
                transposes(r + 1, psum_t, "xt")
                copy_t(r + 1, 0, scopy)
                copy_t(r + 1, 1, vcopy)
                copy_t(r + 1, 2, scopy)
                copy_t(r + 1, 3, vcopy)
            passes(r)
            if not last:
                copy_o(r, 0, vcopy)
                copy_o(r, 1, scopy)
                if r == ROUNDS - 2:
                    store(r * R, 2)
                copy_o(r, 2, scopy)
                copy_o(r, 3, scopy)
                if r == ROUNDS - 2:
                    store(r * R + 2, 2)
                elif r >= ROUNDS // 2:
                    store(r * R, R)
                elif r % 2 == 1:
                    store((r - 1) * R, BIG)
                quant(r + 1, 0, R)
            else:
                for i in range(R):
                    copy_o(r, i, scopy if i % 2 else vcopy)
                    store(r * R + i, 1)
